import numpy as np
import ml_dtypes


def mxq(x, axis, fmt="e4m3"):
    dtype, down = {"e4m3": (ml_dtypes.float8_e4m3fn, 7), "e5m2": (ml_dtypes.float8_e5m2, 14)}[fmt]
    v = np.moveaxis(np.asarray(x, np.float32).astype(ml_dtypes.bfloat16).astype(np.float64), axis, -1)
    blocks = v.reshape(v.shape[:-1] + (-1, 32))
    amax = np.abs(blocks).max(-1, keepdims=True)
    byte = np.maximum(np.where(amax > 0, np.frexp(amax)[1] - 1 + 127, 0) - down, 1)
    scale = np.exp2(byte - 127.0)
    codes = (blocks / scale).astype(np.float32).astype(dtype).astype(np.float64)
    return np.moveaxis((codes * scale).reshape(v.shape), -1, axis)


WIDE = False


def mx_kscale(k):
    if not WIDE:
        return np.ones(k)
    levels = np.array([10, -10, 5, -5, 0])
    a = np.random.permutation(np.resize(levels, k // 512 * 4)).reshape(k // 512, 4)
    idx = np.arange(k)
    return np.exp2(a[idx // 512, idx % 128 // 32])


BF16 = ml_dtypes.bfloat16


def bf(x):
    return np.asarray(x, np.float32).astype(BF16)


def f64(x):
    return np.asarray(x).astype(np.float64)


E2M1 = np.array([0.0, 0.5, 1.0, 1.5, 2.0, 3.0, 4.0, 6.0, -0.0, -0.5, -1.0, -1.5, -2.0, -3.0, -4.0, -6.0])


def pack_weight(w, fmt):
    k, n = w.shape
    w = f64(bf(w)).reshape(k // 32, 32, n)
    amax = np.abs(w).max(1)
    if fmt == "e4m3":
        byte = np.frexp(amax)[1] - 1 + 127 - 7
    else:
        mant, ex = np.frexp(amax / 6.0)
        byte = np.where(mant > 0.5, ex, ex - 1) + 127
    byte = np.clip(np.where(amax > 0, byte, 1), 1, 254)
    scaled = (w * np.exp2(127.0 - byte)[:, None, :]).reshape(k, n).astype(np.float32)
    by_word = np.ascontiguousarray(scaled.reshape(k // 512, 128, 4, n).transpose(0, 1, 3, 2))
    if fmt == "e4m3":
        words = by_word.astype(ml_dtypes.float8_e4m3fn).view(np.uint8)
    else:
        c = by_word.astype(ml_dtypes.float4_e2m1fn).view(np.uint8) & 0xF
        words = c[..., 0::2] | (c[..., 1::2] << 4)
    return np.ascontiguousarray(words), np.ascontiguousarray(byte.astype(np.uint8).reshape(k // 512, 16, n))


def unpack_weight(words, scales, fmt):
    g, p, n, _ = words.shape
    if fmt == "e4m3":
        vals = np.ascontiguousarray(words).view(ml_dtypes.float8_e4m3fn).astype(np.float64)
    else:
        nib = np.empty((g, p, n, 4), np.uint8)
        nib[..., 0::2] = words & 0xF
        nib[..., 1::2] = words >> 4
        vals = E2M1[nib]
    vals = vals * np.repeat(np.exp2(scales.astype(np.float64) - 127.0), 8, axis=1)[..., None]
    return vals.transpose(0, 1, 3, 2).reshape(g * 512, n)

def pack4(w):
    words, scales = pack_weight(w, "e2m1")
    return words.reshape(words.shape[0], 128, -1), scales


def unpack4(words, scales):
    return unpack_weight(words.reshape(words.shape[0], 128, -1, 2), scales, "e2m1")


B, S, DIM, H, NOPE, ROPE_D, VD = 2, 64, 512, 16, 64, 64, 128
QKD = NOPE + ROPE_D
BASE = 10000.0


def rope_cos_sin(seq_len):
    theta = 1.0 / BASE ** (f64(np.arange(0, ROPE_D, 2)) / ROPE_D)
    pos = f64(np.arange(seq_len))
    ang = pos[:, None] * theta[None, :]
    return np.cos(ang), np.sin(ang)


def apply_rope(v, cos, sin):
    b, s, h, d = v.shape
    vs = v.reshape(b, s, h, d // 2, 2)
    c = cos[None, :, None, :]
    sn = sin[None, :, None, :]
    out = np.stack([vs[..., 0] * c - vs[..., 1] * sn, vs[..., 1] * c + vs[..., 0] * sn], axis=-1)
    return out.reshape(b, s, h, d)


def setup_inputs():
    s = mx_kscale(DIM)
    x = bf(np.random.standard_normal((B, S, DIM)) * s)
    Wq_words, Wq_scales = pack4(np.random.standard_normal((DIM, H * QKD)) / np.sqrt(DIM) / s[:, None])
    Wk_words, Wk_scales = pack4(np.random.standard_normal((DIM, H * QKD)) / np.sqrt(DIM) / s[:, None])
    return {'x': x,
            'Wq_words': Wq_words, 'Wq_scales': Wq_scales,
            'Wk_words': Wk_words, 'Wk_scales': Wk_scales}


def reference(x, Wq_words, Wq_scales, Wk_words, Wk_scales):
    xq = mxq(f64(x), 2, 'e4m3')
    q = (xq @ unpack4(Wq_words, Wq_scales)).reshape(B, S, H, QKD)
    k = (xq @ unpack4(Wk_words, Wk_scales)).reshape(B, S, H, QKD)
    cos, sin = rope_cos_sin(S)
    q = np.concatenate([q[..., :NOPE], apply_rope(q[..., NOPE:], cos, sin)], axis=-1)
    k = np.concatenate([k[..., :NOPE], apply_rope(k[..., NOPE:], cos, sin)], axis=-1)
    return q, k

@@ -1,0 +1,161 @@
+import math
+from contextlib import ExitStack
+
+import concourse.mybir as mybir
+from concourse.masks import make_identity
+
+F32 = mybir.dt.float32
+BF16 = mybir.dt.bfloat16
+I32 = mybir.dt.int32
+U32 = mybir.dt.uint32
+U8 = mybir.dt.uint8
+FP8X4 = mybir.dt.float8_e4m3fn_x4
+FP4X4 = mybir.dt.float4_e2m1fn_x4
+ALU = mybir.AluOpType
+ACT = mybir.ActivationFunctionType
+
+P = 128
+SEQUENCES = 2
+POSITIONS = 64
+DIM = 512
+HEADS = 16
+HEAD_DIM = 128
+PLAIN = 64
+PAIRS = 32
+DOUBLINGS = 5
+FEATURES = HEADS * HEAD_DIM
+BANK_COLS = 512
+BANK_HEADS = BANK_COLS // HEAD_DIM
+BANKS = FEATURES // BANK_COLS
+SCALE_ROWS = 4
+
+ROPE_BASE = 10000.0
+RATIO = ROPE_BASE ** (-1.0 / PAIRS)
+ROUND_MAGIC = 1.5 * 2.0**23
+
+FLOPS = 2 * P * DIM * 2 * FEATURES
+
+
+def load_weight(nc, words_dram, scales_dram, words, plane):
+    nc.vector.memset(plane.bitcast(I32), 0)
+    for quadrant in range(P // 32):
+        rows = slice(SCALE_ROWS * quadrant, SCALE_ROWS * (quadrant + 1))
+        nc.sync.dma_start(
+            out=plane[32 * quadrant : 32 * quadrant + SCALE_ROWS, :].bitcast(I32),
+            in_=scales_dram[0, rows, :].bitcast(I32),
+        )
+    nc.sync.dma_start(out=words.bitcast(I32), in_=words_dram[0].bitcast(I32))
+
+
+def build_rotation_table(nc, consts):
+    shape = [P, 2, PAIRS, 2]
+    freq = consts.tile(shape, F32)
+    nc.vector.memset(freq[:, :, 0:1, :], 1.0)
+    nc.vector.memset(freq[:, 0:1, 0:1, 1:2], -1.0)
+    for doubling in range(DOUBLINGS):
+        known = 2**doubling
+        nc.vector.tensor_scalar_mul(
+            out=freq[:, :, known : 2 * known, :], in0=freq[:, :, 0:known, :], scalar1=RATIO**known
+        )
+
+    phase = consts.tile(shape, F32)
+    nc.gpsimd.memset(phase[:], 0.0)
+    nc.gpsimd.memset(phase[:, 0:1, :, 0:1], 0.25)
+    nc.gpsimd.memset(phase[:, 1:2, :, 1:2], 0.25)
+
+    position = consts.tile([P, 1], I32)
+    for s in range(SEQUENCES):
+        nc.gpsimd.iota(
+            position[s * POSITIONS : (s + 1) * POSITIONS, :], pattern=[[0, 1]], base=0, channel_multiplier=1
+        )
+    position_turns = consts.tile([P, 1], F32)
+    nc.vector.tensor_scalar_mul(out=position_turns[:], in0=position[:], scalar1=1.0 / (2.0 * math.pi))
+
+    def flat(tile):
+        return tile[:].rearrange("p e i k -> p (e i k)")
+
+    turns = consts.tile(shape, F32)
+    nc.vector.scalar_tensor_tensor(
+        out=flat(turns), in0=flat(freq), scalar=position_turns[:, 0:1], in1=flat(phase), op0=ALU.mult, op1=ALU.add
+    )
+    whole = consts.tile(shape, F32)
+    nc.vector.tensor_scalar(
+        out=flat(whole), in0=flat(turns), scalar1=ROUND_MAGIC, scalar2=ROUND_MAGIC, op0=ALU.add, op1=ALU.subtract
+    )
+    part = consts.tile(shape, F32)
+    nc.vector.tensor_sub(out=flat(part), in0=flat(turns), in1=flat(whole))
+    rot = consts.tile(shape, F32)
+    nc.scalar.activation(out=flat(rot), in_=flat(part), func=ACT.Sin, scale=2.0 * math.pi)
+    return rot
+
+
+def quantise_x(nc, consts, psum, x_sb):
+    identity = consts.tile([P, P], F32)
+    make_identity(nc, identity[:])
+    x_pairs = x_sb[:].bitcast(F32)
+    flipped = psum.tile([P, 2, P], F32, tag="bank")
+    for u in range(2):
+        nc.tensor.transpose(flipped[:, u, :], x_pairs[:, u : DIM // 2 : 2], identity[:])
+    grouped = consts.tile([P, 4 * P], BF16, align_bytes=64)
+    nc.vector.tensor_copy(
+        out=grouped[:].bitcast(F32).rearrange("p (r u) -> p r u", u=2),
+        in_=flipped[:].rearrange("p u r -> p r u"),
+    )
+    x_words = consts.tile([P, P], U32, align_bytes=64)
+    x_plane = consts.tile([P, P], U8, align_bytes=64)
+    nc.vector.quantize_mx(out=x_words[:].bitcast(FP8X4), scales=x_plane[:], in_=grouped[:])
+    return x_words, x_plane
+
+
+def tile_mla_pa_s_kernel(tc, x, Wq_words, Wq_scales, Wk_words, Wk_scales, out_0, out_1):
+    nc = tc.nc
+    with ExitStack() as ctx:
+        consts = ctx.enter_context(tc.tile_pool(name="consts", bufs=1))
+        products = ctx.enter_context(tc.tile_pool(name="products", bufs=4))
+        results = ctx.enter_context(tc.tile_pool(name="results", bufs=2 * BANKS))
+        psum = ctx.enter_context(tc.psum_pool(name="psum", bufs=8))
+
+        x_sb = consts.tile([P, DIM], BF16)
+        nc.sync.dma_start(out=x_sb[:], in_=x.flatten_outer_dims())
+        w_words = consts.tile([P, 2, 2 * FEATURES], U8, align_bytes=64)
+        w_planes = consts.tile([P, 2, FEATURES], U8, align_bytes=64)
+        load_weight(nc, Wq_words, Wq_scales, w_words[:, 0, :], w_planes[:, 0, :])
+        load_weight(nc, Wk_words, Wk_scales, w_words[:, 1, :], w_planes[:, 1, :])
+
+        rot = build_rotation_table(nc, consts)
+        x_words, x_plane = quantise_x(nc, consts, psum, x_sb)
+
+        for w, out in enumerate((out_0, out_1)):
+            out_rows = out.rearrange("b s h d -> (b s) (h d)")
+            for c in range(BANKS):
+                acc = psum.tile([P, BANK_HEADS, HEAD_DIM], F32, tag="bank")
+                nc.tensor.matmul_mx(
+                    out=acc[:].rearrange("p h d -> p (h d)"),
+                    lhsT=x_words[:].bitcast(FP8X4),
+                    lhsT_scale=x_plane[:],
+                    rhs=w_words[:, w, 2 * BANK_COLS * c : 2 * BANK_COLS * (c + 1)].bitcast(FP4X4),
+                    rhs_scale=w_planes[:, w, BANK_COLS * c : BANK_COLS * (c + 1)],
+                    start=True,
+                    stop=True,
+                )
+                wide = [P, 2, BANK_HEADS, 2 * PAIRS]
+                prod = products.tile(wide, F32)
+                nc.vector.tensor_tensor(
+                    out=prod[:],
+                    in0=acc[:, :, PLAIN:HEAD_DIM].unsqueeze(1).to_broadcast(wide),
+                    in1=rot[:].rearrange("p e i k -> p e (i k)").unsqueeze(2).to_broadcast(wide),
+                    op=ALU.mult,
+                )
+                result = results.tile([P, BANK_HEADS, HEAD_DIM], F32)
+                nc.scalar.copy(out=result[:, :, 0:PLAIN], in_=acc[:, :, 0:PLAIN])
+                terms = prod[:].rearrange("p e h (i k) -> p k h i e", k=2)
+                nc.gpsimd.tensor_tensor(
+                    out=result[:, :, PLAIN:HEAD_DIM].rearrange("p h (i e) -> p h i e", e=2),
+                    in0=terms[:, 0],
+                    in1=terms[:, 1],
+                    op=ALU.add,
+                )
+                nc.sync.dma_start(
+                    out=out_rows[:, BANK_COLS * c : BANK_COLS * (c + 1)],
+                    in_=result[:].rearrange("p h d -> p (h d)"),
+                )

@@ -36,15 +36,18 @@ ROUND_MAGIC = 1.5 * 2.0**23
 FLOPS = 2 * P * DIM * 2 * FEATURES
 
 
-def load_weight(nc, words_dram, scales_dram, words, plane):
-    nc.vector.memset(plane.bitcast(I32), 0)
+def load_words(nc, words_dram, words, first_bank, end_bank):
+    cols = slice(2 * BANK_COLS * first_bank, 2 * BANK_COLS * end_bank)
+    nc.sync.dma_start(out=words[:, cols].bitcast(I32), in_=words_dram[0, :, cols].bitcast(I32))
+
+
+def load_scales(nc, scales_dram, plane):
     for quadrant in range(P // 32):
         rows = slice(SCALE_ROWS * quadrant, SCALE_ROWS * (quadrant + 1))
         nc.sync.dma_start(
             out=plane[32 * quadrant : 32 * quadrant + SCALE_ROWS, :].bitcast(I32),
             in_=scales_dram[0, rows, :].bitcast(I32),
         )
-    nc.sync.dma_start(out=words.bitcast(I32), in_=words_dram[0].bitcast(I32))
 
 
 def build_rotation_table(nc, consts):
@@ -119,8 +122,13 @@ def tile_mla_pa_s_kernel(tc, x, Wq_words, Wq_scales, Wk_words, Wk_scales, out_0,
         nc.sync.dma_start(out=x_sb[:], in_=x.flatten_outer_dims())
         w_words = consts.tile([P, 2, 2 * FEATURES], U8, align_bytes=64)
         w_planes = consts.tile([P, 2, FEATURES], U8, align_bytes=64)
-        load_weight(nc, Wq_words, Wq_scales, w_words[:, 0, :], w_planes[:, 0, :])
-        load_weight(nc, Wk_words, Wk_scales, w_words[:, 1, :], w_planes[:, 1, :])
+        nc.vector.memset(w_planes[:, 0, :].bitcast(I32), 0)
+        nc.gpsimd.memset(w_planes[:, 1, :].bitcast(F32), 0.0)
+        load_words(nc, Wq_words, w_words[:, 0, :], 0, 1)
+        load_scales(nc, Wq_scales, w_planes[:, 0, :])
+        load_words(nc, Wq_words, w_words[:, 0, :], 1, BANKS)
+        load_words(nc, Wk_words, w_words[:, 1, :], 0, BANKS)
+        load_scales(nc, Wk_scales, w_planes[:, 1, :])
 
         rot = build_rotation_table(nc, consts)
         x_words, x_plane = quantise_x(nc, consts, psum, x_sb)

@@ -22,12 +22,13 @@ HEADS = 16
 HEAD_DIM = 128
 PLAIN = 64
 PAIRS = 32
-DOUBLINGS = 5
 FEATURES = HEADS * HEAD_DIM
 BANK_COLS = 512
 BANK_HEADS = BANK_COLS // HEAD_DIM
 BANKS = FEATURES // BANK_COLS
 SCALE_ROWS = 4
+BLOCKS = 2 * BANKS
+GPSIMD_SUMS = 6
 
 ROPE_BASE = 10000.0
 RATIO = ROPE_BASE ** (-1.0 / PAIRS)
@@ -50,120 +51,129 @@ def load_scales(nc, scales_dram, plane):
         )
 
 
-def build_rotation_table(nc, consts):
-    shape = [P, 2, PAIRS, 2]
-    freq = consts.tile(shape, F32)
-    nc.vector.memset(freq[:, :, 0:1, :], 1.0)
-    nc.vector.memset(freq[:, 0:1, 0:1, 1:2], -1.0)
-    for doubling in range(DOUBLINGS):
-        known = 2**doubling
-        nc.vector.tensor_scalar_mul(
-            out=freq[:, :, known : 2 * known, :], in0=freq[:, :, 0:known, :], scalar1=RATIO**known
-        )
-
-    phase = consts.tile(shape, F32)
-    nc.gpsimd.memset(phase[:], 0.0)
-    nc.gpsimd.memset(phase[:, 0:1, :, 0:1], 0.25)
-    nc.gpsimd.memset(phase[:, 1:2, :, 1:2], 0.25)
-
-    position = consts.tile([P, 1], I32)
-    for s in range(SEQUENCES):
-        nc.gpsimd.iota(
-            position[s * POSITIONS : (s + 1) * POSITIONS, :], pattern=[[0, 1]], base=0, channel_multiplier=1
-        )
-    position_turns = consts.tile([P, 1], F32)
-    nc.vector.tensor_scalar_mul(out=position_turns[:], in0=position[:], scalar1=1.0 / (2.0 * math.pi))
-
-    def flat(tile):
-        return tile[:].rearrange("p e i k -> p (e i k)")
-
-    turns = consts.tile(shape, F32)
-    nc.vector.scalar_tensor_tensor(
-        out=flat(turns), in0=flat(freq), scalar=position_turns[:, 0:1], in1=flat(phase), op0=ALU.mult, op1=ALU.add
-    )
-    whole = consts.tile(shape, F32)
-    nc.vector.tensor_scalar(
-        out=flat(whole), in0=flat(turns), scalar1=ROUND_MAGIC, scalar2=ROUND_MAGIC, op0=ALU.add, op1=ALU.subtract
-    )
-    part = consts.tile(shape, F32)
-    nc.vector.tensor_sub(out=flat(part), in0=flat(turns), in1=flat(whole))
-    rot = consts.tile(shape, F32)
-    nc.scalar.activation(out=flat(rot), in_=flat(part), func=ACT.Sin, scale=2.0 * math.pi)
-    return rot
-
-
-def quantise_x(nc, consts, psum, x_sb):
-    identity = consts.tile([P, P], F32)
-    make_identity(nc, identity[:])
-    x_pairs = x_sb[:].bitcast(F32)
-    flipped = psum.tile([P, 2, P], F32, tag="bank")
-    for u in range(2):
-        nc.tensor.transpose(flipped[:, u, :], x_pairs[:, u : DIM // 2 : 2], identity[:])
-    grouped = consts.tile([P, 4 * P], BF16, align_bytes=64)
-    nc.vector.tensor_copy(
-        out=grouped[:].bitcast(F32).rearrange("p (r u) -> p r u", u=2),
-        in_=flipped[:].rearrange("p u r -> p r u"),
-    )
-    x_words = consts.tile([P, P], U32, align_bytes=64)
-    x_plane = consts.tile([P, P], U8, align_bytes=64)
-    nc.vector.quantize_mx(out=x_words[:].bitcast(FP8X4), scales=x_plane[:], in_=grouped[:])
-    return x_words, x_plane
-
-
 def tile_mla_pa_s_kernel(tc, x, Wq_words, Wq_scales, Wk_words, Wk_scales, out_0, out_1):
     nc = tc.nc
     with ExitStack() as ctx:
+        ctx.enter_context(tc.manual_schedule())
         consts = ctx.enter_context(tc.tile_pool(name="consts", bufs=1))
-        products = ctx.enter_context(tc.tile_pool(name="products", bufs=4))
-        results = ctx.enter_context(tc.tile_pool(name="results", bufs=2 * BANKS))
+        products = ctx.enter_context(tc.tile_pool(name="products", bufs=BLOCKS))
+        results = ctx.enter_context(tc.tile_pool(name="results", bufs=BLOCKS))
         psum = ctx.enter_context(tc.psum_pool(name="psum", bufs=8))
 
         x_sb = consts.tile([P, DIM], BF16)
-        nc.sync.dma_start(out=x_sb[:], in_=x.flatten_outer_dims())
         w_words = consts.tile([P, 2, 2 * FEATURES], U8, align_bytes=64)
         w_planes = consts.tile([P, 2, FEATURES], U8, align_bytes=64)
-        nc.vector.memset(w_planes[:, 0, :].bitcast(I32), 0)
-        nc.gpsimd.memset(w_planes[:, 1, :].bitcast(F32), 0.0)
+        position = consts.tile([P, 1], I32)
+        identity = consts.tile([P, P], F32)
+        nc.sync.dma_start(out=x_sb[:], in_=x.flatten_outer_dims())
         load_words(nc, Wq_words, w_words[:, 0, :], 0, 1)
+        nc.vector.memset(w_planes[:, 0, :].bitcast(I32), 0)
         load_scales(nc, Wq_scales, w_planes[:, 0, :])
         load_words(nc, Wq_words, w_words[:, 0, :], 1, BANKS)
         load_words(nc, Wk_words, w_words[:, 1, :], 0, BANKS)
+        for s in range(SEQUENCES):
+            nc.gpsimd.iota(
+                position[s * POSITIONS : (s + 1) * POSITIONS, :], pattern=[[0, 1]], base=0, channel_multiplier=1
+            )
+        make_identity(nc, identity[:])
+
+        table = [P, 2, PAIRS, 2]
+        freq = consts.tile(table, F32)
+        phase = consts.tile(table, F32)
+        position_turns = consts.tile([P, 1], F32)
+
+        def double_freq(known):
+            nc.vector.tensor_scalar_mul(
+                out=freq[:, :, known : 2 * known, :], in0=freq[:, :, 0:known, :], scalar1=RATIO**known
+            )
+
+        nc.vector.memset(freq[:, :, 0:1, :], 1.0)
+        nc.vector.memset(freq[:, 0:1, 0:1, 1:2], -1.0)
+        nc.vector.memset(phase[:], 0.0)
+        double_freq(1)
+        nc.vector.memset(phase[:, 0:1, :, 0:1], 0.25)
+        double_freq(2)
+        nc.vector.memset(phase[:, 1:2, :, 1:2], 0.25)
+        double_freq(4)
+        nc.vector.memset(w_planes[:, 1, :].bitcast(I32), 0)
         load_scales(nc, Wk_scales, w_planes[:, 1, :])
+        double_freq(8)
+        nc.vector.tensor_scalar_mul(out=position_turns[:], in0=position[:], scalar1=1.0 / (2.0 * math.pi))
+        double_freq(16)
 
-        rot = build_rotation_table(nc, consts)
-        x_words, x_plane = quantise_x(nc, consts, psum, x_sb)
+        def flat(tile):
+            return tile[:].rearrange("p e i k -> p (e i k)")
 
-        for w, out in enumerate((out_0, out_1)):
-            out_rows = out.rearrange("b s h d -> (b s) (h d)")
-            for c in range(BANKS):
-                acc = psum.tile([P, BANK_HEADS, HEAD_DIM], F32, tag="bank")
-                nc.tensor.matmul_mx(
-                    out=acc[:].rearrange("p h d -> p (h d)"),
-                    lhsT=x_words[:].bitcast(FP8X4),
-                    lhsT_scale=x_plane[:],
-                    rhs=w_words[:, w, 2 * BANK_COLS * c : 2 * BANK_COLS * (c + 1)].bitcast(FP4X4),
-                    rhs_scale=w_planes[:, w, BANK_COLS * c : BANK_COLS * (c + 1)],
-                    start=True,
-                    stop=True,
-                )
-                wide = [P, 2, BANK_HEADS, 2 * PAIRS]
-                prod = products.tile(wide, F32)
-                nc.vector.tensor_tensor(
-                    out=prod[:],
-                    in0=acc[:, :, PLAIN:HEAD_DIM].unsqueeze(1).to_broadcast(wide),
-                    in1=rot[:].rearrange("p e i k -> p e (i k)").unsqueeze(2).to_broadcast(wide),
-                    op=ALU.mult,
-                )
-                result = results.tile([P, BANK_HEADS, HEAD_DIM], F32)
-                nc.scalar.copy(out=result[:, :, 0:PLAIN], in_=acc[:, :, 0:PLAIN])
-                terms = prod[:].rearrange("p e h (i k) -> p k h i e", k=2)
-                nc.gpsimd.tensor_tensor(
-                    out=result[:, :, PLAIN:HEAD_DIM].rearrange("p h (i e) -> p h i e", e=2),
-                    in0=terms[:, 0],
-                    in1=terms[:, 1],
-                    op=ALU.add,
-                )
-                nc.sync.dma_start(
-                    out=out_rows[:, BANK_COLS * c : BANK_COLS * (c + 1)],
-                    in_=result[:].rearrange("p h d -> p (h d)"),
-                )
+        turns = consts.tile(table, F32)
+        nc.vector.scalar_tensor_tensor(
+            out=flat(turns), in0=flat(freq), scalar=position_turns[:, 0:1], in1=flat(phase), op0=ALU.mult, op1=ALU.add
+        )
+        whole = consts.tile(table, F32)
+        nc.vector.tensor_scalar(
+            out=flat(whole), in0=flat(turns), scalar1=ROUND_MAGIC, scalar2=ROUND_MAGIC, op0=ALU.add, op1=ALU.subtract
+        )
+
+        x_pairs = x_sb[:].bitcast(F32)
+        flipped = psum.tile([P, 2, P], F32, tag="bank")
+        for u in range(2):
+            nc.tensor.transpose(flipped[:, u, :], x_pairs[:, u : DIM // 2 : 2], identity[:])
+        grouped = consts.tile([P, 4 * P], BF16, align_bytes=64)
+        nc.vector.tensor_copy(
+            out=grouped[:].bitcast(F32).rearrange("p (r u) -> p r u", u=2),
+            in_=flipped[:].rearrange("p u r -> p r u"),
+        )
+
+        part = consts.tile(table, F32)
+        nc.vector.tensor_sub(out=flat(part), in0=flat(turns), in1=flat(whole))
+        rot = consts.tile(table, F32)
+        nc.scalar.activation(out=flat(rot), in_=flat(part), func=ACT.Sin, scale=2.0 * math.pi)
+
+        x_words = consts.tile([P, P], U32, align_bytes=64)
+        x_plane = consts.tile([P, P], U8, align_bytes=64)
+        nc.vector.quantize_mx(out=x_words[:].bitcast(FP8X4), scales=x_plane[:], in_=grouped[:])
+
+        out_rows = [out.rearrange("b s h d -> (b s) (h d)") for out in (out_0, out_1)]
+        wide = [P, 2, BANK_HEADS, 2 * PAIRS]
+
+        def sum_and_store(engine, block, prod, result):
+            w, c = divmod(block, BANKS)
+            terms = prod[:].rearrange("p e h (i k) -> p k h i e", k=2)
+            engine.tensor_tensor(
+                out=result[:, :, PLAIN:HEAD_DIM].rearrange("p h (i e) -> p h i e", e=2),
+                in0=terms[:, 0],
+                in1=terms[:, 1],
+                op=ALU.add,
+            )
+            nc.sync.dma_start(
+                out=out_rows[w][:, BANK_COLS * c : BANK_COLS * (c + 1)],
+                in_=result[:].rearrange("p h d -> p (h d)"),
+            )
+
+        owed = []
+        for block in range(BLOCKS):
+            w, c = divmod(block, BANKS)
+            acc = psum.tile([P, BANK_HEADS, HEAD_DIM], F32, tag="bank")
+            nc.tensor.matmul_mx(
+                out=acc[:].rearrange("p h d -> p (h d)"),
+                lhsT=x_words[:].bitcast(FP8X4),
+                lhsT_scale=x_plane[:],
+                rhs=w_words[:, w, 2 * BANK_COLS * c : 2 * BANK_COLS * (c + 1)].bitcast(FP4X4),
+                rhs_scale=w_planes[:, w, BANK_COLS * c : BANK_COLS * (c + 1)],
+                start=True,
+                stop=True,
+            )
+            prod = products.tile(wide, F32)
+            nc.vector.tensor_tensor(
+                out=prod[:],
+                in0=acc[:, :, PLAIN:HEAD_DIM].unsqueeze(1).to_broadcast(wide),
+                in1=rot[:].rearrange("p e i k -> p e (i k)").unsqueeze(2).to_broadcast(wide),
+                op=ALU.mult,
+            )
+            result = results.tile([P, BANK_HEADS, HEAD_DIM], F32)
+            nc.scalar.copy(out=result[:, :, 0:PLAIN], in_=acc[:, :, 0:PLAIN])
+            if block < GPSIMD_SUMS:
+                sum_and_store(nc.gpsimd, block, prod, result)
+            else:
+                owed.append((block, prod, result))
+        for late in owed:
+            sum_and_store(nc.vector, *late)

@@ -28,7 +28,7 @@ BANK_HEADS = BANK_COLS // HEAD_DIM
 BANKS = FEATURES // BANK_COLS
 SCALE_ROWS = 4
 BLOCKS = 2 * BANKS
-GPSIMD_SUMS = 6
+GPSIMD_SUMS = 5
 
 ROPE_BASE = 10000.0
 RATIO = ROPE_BASE ** (-1.0 / PAIRS)

@@ -28,6 +28,8 @@ BANK_HEADS = BANK_COLS // HEAD_DIM
 BANKS = FEATURES // BANK_COLS
 SCALE_ROWS = 4
 BLOCKS = 2 * BANKS
+WARM_BEFORE = 4
+WARM_AFTER = 2
 GPSIMD_SUMS = 5
 
 ROPE_BASE = 10000.0
@@ -66,6 +68,15 @@ def tile_mla_pa_s_kernel(tc, x, Wq_words, Wq_scales, Wk_words, Wk_scales, out_0,
         position = consts.tile([P, 1], I32)
         identity = consts.tile([P, P], F32)
         nc.sync.dma_start(out=x_sb[:], in_=x.flatten_outer_dims())
+        warm = consts.tile([P, P], F32)
+        nc.gpsimd.memset(warm[:], 0.0)
+        idle = psum.tile([P, P], F32, tag="bank")
+
+        def keep_busy(count):
+            for unused in range(count):
+                nc.tensor.matmul(out=idle[:], lhsT=warm[:], rhs=warm[:], start=True, stop=True)
+
+        keep_busy(WARM_BEFORE)
         load_words(nc, Wq_words, w_words[:, 0, :], 0, 1)
         nc.vector.memset(w_planes[:, 0, :].bitcast(I32), 0)
         load_scales(nc, Wq_scales, w_planes[:, 0, :])
@@ -117,6 +128,7 @@ def tile_mla_pa_s_kernel(tc, x, Wq_words, Wq_scales, Wk_words, Wk_scales, out_0,
         flipped = psum.tile([P, 2, P], F32, tag="bank")
         for u in range(2):
             nc.tensor.transpose(flipped[:, u, :], x_pairs[:, u : DIM // 2 : 2], identity[:])
+        keep_busy(WARM_AFTER)
         grouped = consts.tile([P, 4 * P], BF16, align_bytes=64)
         nc.vector.tensor_copy(
             out=grouped[:].bitcast(F32).rearrange("p (r u) -> p r u", u=2),

@@ -30,7 +30,7 @@ SCALE_ROWS = 4
 BLOCKS = 2 * BANKS
 WARM_BEFORE = 4
 WARM_AFTER = 2
-GPSIMD_SUMS = 5
+GPSIMD_SUMS = 4
 
 ROPE_BASE = 10000.0
 RATIO = ROPE_BASE ** (-1.0 / PAIRS)

@@ -30,6 +30,7 @@ SCALE_ROWS = 4
 BLOCKS = 2 * BANKS
 WARM_BEFORE = 4
 WARM_AFTER = 2
+VECTOR_SUMS_FROM = 6
 GPSIMD_SUMS = 4
 
 ROPE_BASE = 10000.0
@@ -187,5 +188,7 @@ def tile_mla_pa_s_kernel(tc, x, Wq_words, Wq_scales, Wk_words, Wk_scales, out_0,
                 sum_and_store(nc.gpsimd, block, prod, result)
             else:
                 owed.append((block, prod, result))
-        for late in owed:
-            sum_and_store(nc.vector, *late)
+            if block >= VECTOR_SUMS_FROM:
+                for late in owed:
+                    sum_and_store(nc.vector, *late)
+                owed.clear()

@@ -28,6 +28,7 @@ BANK_HEADS = BANK_COLS // HEAD_DIM
 BANKS = FEATURES // BANK_COLS
 SCALE_ROWS = 4
 BLOCKS = 2 * BANKS
+FIRST_PIECES = 4
 WARM_BEFORE = 4
 WARM_AFTER = 2
 VECTOR_SUMS_FROM = 6
@@ -165,25 +166,32 @@ def tile_mla_pa_s_kernel(tc, x, Wq_words, Wq_scales, Wk_words, Wk_scales, out_0,
         owed = []
         for block in range(BLOCKS):
             w, c = divmod(block, BANKS)
-            acc = psum.tile([P, BANK_HEADS, HEAD_DIM], F32, tag="bank")
-            nc.tensor.matmul_mx(
-                out=acc[:].rearrange("p h d -> p (h d)"),
-                lhsT=x_words[:].bitcast(FP8X4),
-                lhsT_scale=x_plane[:],
-                rhs=w_words[:, w, 2 * BANK_COLS * c : 2 * BANK_COLS * (c + 1)].bitcast(FP4X4),
-                rhs_scale=w_planes[:, w, BANK_COLS * c : BANK_COLS * (c + 1)],
-                start=True,
-                stop=True,
-            )
             prod = products.tile(wide, F32)
-            nc.vector.tensor_tensor(
-                out=prod[:],
-                in0=acc[:, :, PLAIN:HEAD_DIM].unsqueeze(1).to_broadcast(wide),
-                in1=rot[:].rearrange("p e i k -> p e (i k)").unsqueeze(2).to_broadcast(wide),
-                op=ALU.mult,
-            )
             result = results.tile([P, BANK_HEADS, HEAD_DIM], F32)
-            nc.scalar.copy(out=result[:, :, 0:PLAIN], in_=acc[:, :, 0:PLAIN])
+            pieces = FIRST_PIECES if block == 0 else 1
+            heads = BANK_HEADS // pieces
+            for piece in range(pieces):
+                first = BANK_COLS * c + HEAD_DIM * heads * piece
+                end = first + HEAD_DIM * heads
+                mine = slice(heads * piece, heads * (piece + 1))
+                acc = psum.tile([P, heads, HEAD_DIM], F32, tag="bank")
+                nc.tensor.matmul_mx(
+                    out=acc[:].rearrange("p h d -> p (h d)"),
+                    lhsT=x_words[:].bitcast(FP8X4),
+                    lhsT_scale=x_plane[:],
+                    rhs=w_words[:, w, 2 * first : 2 * end].bitcast(FP4X4),
+                    rhs_scale=w_planes[:, w, first:end],
+                    start=True,
+                    stop=True,
+                )
+                shape = [P, 2, heads, 2 * PAIRS]
+                nc.vector.tensor_tensor(
+                    out=prod[:, :, mine, :],
+                    in0=acc[:, :, PLAIN:HEAD_DIM].unsqueeze(1).to_broadcast(shape),
+                    in1=rot[:].rearrange("p e i k -> p e (i k)").unsqueeze(2).to_broadcast(shape),
+                    op=ALU.mult,
+                )
+                nc.scalar.copy(out=result[:, mine, 0:PLAIN], in_=acc[:, :, 0:PLAIN])
             if block < GPSIMD_SUMS:
                 sum_and_store(nc.gpsimd, block, prod, result)
             else:

@@ -79,6 +79,8 @@ def tile_mla_pa_s_kernel(tc, x, Wq_words, Wq_scales, Wk_words, Wk_scales, out_0,
                 nc.tensor.matmul(out=idle[:], lhsT=warm[:], rhs=warm[:], start=True, stop=True)
 
         keep_busy(WARM_BEFORE)
+        primed = consts.tile([P, 1], F32)
+        nc.scalar.activation(out=primed[:], in_=warm[:, 0:1], func=ACT.Sin)
         load_words(nc, Wq_words, w_words[:, 0, :], 0, 1)
         nc.vector.memset(w_planes[:, 0, :].bitcast(I32), 0)
         load_scales(nc, Wq_scales, w_planes[:, 0, :])
@@ -131,14 +133,14 @@ def tile_mla_pa_s_kernel(tc, x, Wq_words, Wq_scales, Wk_words, Wk_scales, out_0,
         for u in range(2):
             nc.tensor.transpose(flipped[:, u, :], x_pairs[:, u : DIM // 2 : 2], identity[:])
         keep_busy(WARM_AFTER)
+        part = consts.tile(table, F32)
+        nc.vector.tensor_sub(out=flat(part), in0=flat(turns), in1=flat(whole))
+
         grouped = consts.tile([P, 4 * P], BF16, align_bytes=64)
-        nc.vector.tensor_copy(
+        nc.scalar.copy(
             out=grouped[:].bitcast(F32).rearrange("p (r u) -> p r u", u=2),
             in_=flipped[:].rearrange("p u r -> p r u"),
         )
-
-        part = consts.tile(table, F32)
-        nc.vector.tensor_sub(out=flat(part), in0=flat(turns), in1=flat(whole))
         rot = consts.tile(table, F32)
         nc.scalar.activation(out=flat(rot), in_=flat(part), func=ACT.Sin, scale=2.0 * math.pi)
 

@@ -29,6 +29,7 @@ BANKS = FEATURES // BANK_COLS
 SCALE_ROWS = 4
 BLOCKS = 2 * BANKS
 FIRST_PIECES = 4
+LAST_PIECES = 2
 WARM_BEFORE = 4
 WARM_AFTER = 2
 VECTOR_SUMS_FROM = 6
@@ -151,54 +152,76 @@ def tile_mla_pa_s_kernel(tc, x, Wq_words, Wq_scales, Wk_words, Wk_scales, out_0,
         out_rows = [out.rearrange("b s h d -> (b s) (h d)") for out in (out_0, out_1)]
         wide = [P, 2, BANK_HEADS, 2 * PAIRS]
 
-        def sum_and_store(engine, block, prod, result):
+        def project(block, first_head, heads):
             w, c = divmod(block, BANKS)
-            terms = prod[:].rearrange("p e h (i k) -> p k h i e", k=2)
+            first = BANK_COLS * c + HEAD_DIM * first_head
+            end = first + HEAD_DIM * heads
+            acc = psum.tile([P, heads, HEAD_DIM], F32, tag="bank")
+            nc.tensor.matmul_mx(
+                out=acc[:].rearrange("p h d -> p (h d)"),
+                lhsT=x_words[:].bitcast(FP8X4),
+                lhsT_scale=x_plane[:],
+                rhs=w_words[:, w, 2 * first : 2 * end].bitcast(FP4X4),
+                rhs_scale=w_planes[:, w, first:end],
+                start=True,
+                stop=True,
+            )
+            return acc
+
+        def multiply(acc, prod, heads):
+            shape = [P, 2, heads, 2 * PAIRS]
+            nc.vector.tensor_tensor(
+                out=prod,
+                in0=acc[:, :, PLAIN:HEAD_DIM].unsqueeze(1).to_broadcast(shape),
+                in1=rot[:].rearrange("p e i k -> p e (i k)").unsqueeze(2).to_broadcast(shape),
+                op=ALU.mult,
+            )
+
+        def sum_and_store(engine, block, prod, result, first_head=0, heads=BANK_HEADS):
+            w, c = divmod(block, BANKS)
+            mine = slice(first_head, first_head + heads)
+            terms = prod[:, :, mine, :].rearrange("p e h (i k) -> p k h i e", k=2)
             engine.tensor_tensor(
-                out=result[:, :, PLAIN:HEAD_DIM].rearrange("p h (i e) -> p h i e", e=2),
+                out=result[:, mine, PLAIN:HEAD_DIM].rearrange("p h (i e) -> p h i e", e=2),
                 in0=terms[:, 0],
                 in1=terms[:, 1],
                 op=ALU.add,
             )
+            first = BANK_COLS * c + HEAD_DIM * first_head
             nc.sync.dma_start(
-                out=out_rows[w][:, BANK_COLS * c : BANK_COLS * (c + 1)],
-                in_=result[:].rearrange("p h d -> p (h d)"),
+                out=out_rows[w][:, first : first + HEAD_DIM * heads],
+                in_=result[:, mine, :].rearrange("p h d -> p (h d)"),
             )
 
         owed = []
         for block in range(BLOCKS):
-            w, c = divmod(block, BANKS)
             prod = products.tile(wide, F32)
             result = results.tile([P, BANK_HEADS, HEAD_DIM], F32)
-            pieces = FIRST_PIECES if block == 0 else 1
-            heads = BANK_HEADS // pieces
-            for piece in range(pieces):
-                first = BANK_COLS * c + HEAD_DIM * heads * piece
-                end = first + HEAD_DIM * heads
-                mine = slice(heads * piece, heads * (piece + 1))
-                acc = psum.tile([P, heads, HEAD_DIM], F32, tag="bank")
-                nc.tensor.matmul_mx(
-                    out=acc[:].rearrange("p h d -> p (h d)"),
-                    lhsT=x_words[:].bitcast(FP8X4),
-                    lhsT_scale=x_plane[:],
-                    rhs=w_words[:, w, 2 * first : 2 * end].bitcast(FP4X4),
-                    rhs_scale=w_planes[:, w, first:end],
-                    start=True,
-                    stop=True,
-                )
-                shape = [P, 2, heads, 2 * PAIRS]
-                nc.vector.tensor_tensor(
-                    out=prod[:, :, mine, :],
-                    in0=acc[:, :, PLAIN:HEAD_DIM].unsqueeze(1).to_broadcast(shape),
-                    in1=rot[:].rearrange("p e i k -> p e (i k)").unsqueeze(2).to_broadcast(shape),
-                    op=ALU.mult,
-                )
-                nc.scalar.copy(out=result[:, mine, 0:PLAIN], in_=acc[:, :, 0:PLAIN])
+            if block == 0:
+                heads = BANK_HEADS // FIRST_PIECES
+                for piece in range(FIRST_PIECES):
+                    mine = slice(heads * piece, heads * (piece + 1))
+                    acc = project(block, heads * piece, heads)
+                    multiply(acc, prod[:, :, mine, :], heads)
+                    nc.scalar.copy(out=result[:, mine, 0:PLAIN], in_=acc[:, :, 0:PLAIN])
+            elif block < BLOCKS - 1:
+                acc = project(block, 0, BANK_HEADS)
+                multiply(acc, prod[:], BANK_HEADS)
+                nc.scalar.copy(out=result[:, :, 0:PLAIN], in_=acc[:, :, 0:PLAIN])
             if block < GPSIMD_SUMS:
                 sum_and_store(nc.gpsimd, block, prod, result)
-            else:
+            elif block < BLOCKS - 1:
                 owed.append((block, prod, result))
-            if block >= VECTOR_SUMS_FROM:
+            if block == VECTOR_SUMS_FROM:
                 for late in owed:
                     sum_and_store(nc.vector, *late)
                 owed.clear()
+            if block == BLOCKS - 1:
+                acc = project(block, 0, BANK_HEADS)
+                nc.scalar.copy(out=result[:, :, 0:PLAIN], in_=acc[:, :, 0:PLAIN])
+                heads = BANK_HEADS // LAST_PIECES
+                for piece in range(LAST_PIECES):
+                    mine = slice(heads * piece, heads * (piece + 1))
+                    multiply(acc[:, mine, :], prod[:, :, mine, :], heads)
+                for piece in range(LAST_PIECES):
+                    sum_and_store(nc.vector, block, prod, result, heads * piece, heads)

@@ -30,7 +30,7 @@ SCALE_ROWS = 4
 BLOCKS = 2 * BANKS
 FIRST_PIECES = 4
 LAST_PIECES = 2
-WARM_BEFORE = 4
+WARM_BEFORE = 2
 WARM_AFTER = 2
 VECTOR_SUMS_FROM = 6
 GPSIMD_SUMS = 4

@@ -71,17 +71,16 @@ def tile_mla_pa_s_kernel(tc, x, Wq_words, Wq_scales, Wk_words, Wk_scales, out_0,
         position = consts.tile([P, 1], I32)
         identity = consts.tile([P, P], F32)
         nc.sync.dma_start(out=x_sb[:], in_=x.flatten_outer_dims())
-        warm = consts.tile([P, P], F32)
-        nc.gpsimd.memset(warm[:], 0.0)
+        make_identity(nc, identity[:])
         idle = psum.tile([P, P], F32, tag="bank")
 
         def keep_busy(count):
             for unused in range(count):
-                nc.tensor.matmul(out=idle[:], lhsT=warm[:], rhs=warm[:], start=True, stop=True)
+                nc.tensor.matmul(out=idle[:], lhsT=identity[:], rhs=identity[:], start=True, stop=True)
 
         keep_busy(WARM_BEFORE)
         primed = consts.tile([P, 1], F32)
-        nc.scalar.activation(out=primed[:], in_=warm[:, 0:1], func=ACT.Sin)
+        nc.scalar.activation(out=primed[:], in_=identity[:, 0:1], func=ACT.Sin)
         load_words(nc, Wq_words, w_words[:, 0, :], 0, 1)
         nc.vector.memset(w_planes[:, 0, :].bitcast(I32), 0)
         load_scales(nc, Wq_scales, w_planes[:, 0, :])
@@ -91,31 +90,31 @@ def tile_mla_pa_s_kernel(tc, x, Wq_words, Wq_scales, Wk_words, Wk_scales, out_0,
             nc.gpsimd.iota(
                 position[s * POSITIONS : (s + 1) * POSITIONS, :], pattern=[[0, 1]], base=0, channel_multiplier=1
             )
-        make_identity(nc, identity[:])
 
         table = [P, 2, PAIRS, 2]
         freq = consts.tile(table, F32)
         phase = consts.tile(table, F32)
         position_turns = consts.tile([P, 1], F32)
 
-        def double_freq(known):
-            nc.vector.tensor_scalar_mul(
-                out=freq[:, :, known : 2 * known, :], in0=freq[:, :, 0:known, :], scalar1=RATIO**known
-            )
+        def spread_freq(known, copies):
+            for j in range(1, copies + 1):
+                nc.vector.tensor_scalar_mul(
+                    out=freq[:, :, j * known : (j + 1) * known, :],
+                    in0=freq[:, :, 0:known, :],
+                    scalar1=RATIO ** (j * known),
+                )
 
         nc.vector.memset(freq[:, :, 0:1, :], 1.0)
         nc.vector.memset(freq[:, 0:1, 0:1, 1:2], -1.0)
         nc.vector.memset(phase[:], 0.0)
-        double_freq(1)
+        spread_freq(1, 3)
         nc.vector.memset(phase[:, 0:1, :, 0:1], 0.25)
-        double_freq(2)
         nc.vector.memset(phase[:, 1:2, :, 1:2], 0.25)
-        double_freq(4)
+        spread_freq(4, 3)
         nc.vector.memset(w_planes[:, 1, :].bitcast(I32), 0)
         load_scales(nc, Wk_scales, w_planes[:, 1, :])
-        double_freq(8)
+        spread_freq(16, 1)
         nc.vector.tensor_scalar_mul(out=position_turns[:], in0=position[:], scalar1=1.0 / (2.0 * math.pi))
-        double_freq(16)
 
         def flat(tile):
             return tile[:].rearrange("p e i k -> p (e i k)")

@@ -29,6 +29,7 @@ BANKS = FEATURES // BANK_COLS
 SCALE_ROWS = 4
 BLOCKS = 2 * BANKS
 FIRST_PIECES = 4
+FIRST_SUM_HEADS = 2
 LAST_PIECES = 2
 WARM_BEFORE = 2
 WARM_AFTER = 2
@@ -203,13 +204,16 @@ def tile_mla_pa_s_kernel(tc, x, Wq_words, Wq_scales, Wk_words, Wk_scales, out_0,
                     acc = project(block, heads * piece, heads)
                     multiply(acc, prod[:, :, mine, :], heads)
                     nc.scalar.copy(out=result[:, mine, 0:PLAIN], in_=acc[:, :, 0:PLAIN])
+                    done = heads * (piece + 1)
+                    if done % FIRST_SUM_HEADS == 0:
+                        sum_and_store(nc.gpsimd, block, prod, result, done - FIRST_SUM_HEADS, FIRST_SUM_HEADS)
             elif block < BLOCKS - 1:
                 acc = project(block, 0, BANK_HEADS)
                 multiply(acc, prod[:], BANK_HEADS)
                 nc.scalar.copy(out=result[:, :, 0:PLAIN], in_=acc[:, :, 0:PLAIN])
-            if block < GPSIMD_SUMS:
+            if 0 < block < GPSIMD_SUMS:
                 sum_and_store(nc.gpsimd, block, prod, result)
-            elif block < BLOCKS - 1:
+            elif GPSIMD_SUMS <= block < BLOCKS - 1:
                 owed.append((block, prod, result))
             if block == VECTOR_SUMS_FROM:
                 for late in owed:

import math
from contextlib import ExitStack

import concourse.mybir as mybir
from concourse.masks import make_identity

F32 = mybir.dt.float32
BF16 = mybir.dt.bfloat16
I32 = mybir.dt.int32
U32 = mybir.dt.uint32
U8 = mybir.dt.uint8
FP8X4 = mybir.dt.float8_e4m3fn_x4
FP4X4 = mybir.dt.float4_e2m1fn_x4
ALU = mybir.AluOpType
ACT = mybir.ActivationFunctionType

P = 128
SEQUENCES = 2
POSITIONS = 64
DIM = 512
HEADS = 16
HEAD_DIM = 128
PLAIN = 64
PAIRS = 32
FEATURES = HEADS * HEAD_DIM
BANK_COLS = 512
BANK_HEADS = BANK_COLS // HEAD_DIM
BANKS = FEATURES // BANK_COLS
SCALE_ROWS = 4
BLOCKS = 2 * BANKS
FIRST_PIECES = 4
FIRST_SUM_HEADS = 2
LAST_PIECES = 2
WARM_BEFORE = 2
WARM_AFTER = 2
VECTOR_SUMS_FROM = 6
GPSIMD_SUMS = 4

ROPE_BASE = 10000.0
RATIO = ROPE_BASE ** (-1.0 / PAIRS)
ROUND_MAGIC = 1.5 * 2.0**23

FLOPS = 2 * P * DIM * 2 * FEATURES


def load_words(nc, words_dram, words, first_bank, end_bank):
    cols = slice(2 * BANK_COLS * first_bank, 2 * BANK_COLS * end_bank)
    nc.sync.dma_start(out=words[:, cols].bitcast(I32), in_=words_dram[0, :, cols].bitcast(I32))


def load_scales(nc, scales_dram, plane):
    for quadrant in range(P // 32):
        rows = slice(SCALE_ROWS * quadrant, SCALE_ROWS * (quadrant + 1))
        nc.sync.dma_start(
            out=plane[32 * quadrant : 32 * quadrant + SCALE_ROWS, :].bitcast(I32),
            in_=scales_dram[0, rows, :].bitcast(I32),
        )


def tile_mla_pa_s_kernel(tc, x, Wq_words, Wq_scales, Wk_words, Wk_scales, out_0, out_1):
    nc = tc.nc
    with ExitStack() as ctx:
        ctx.enter_context(tc.manual_schedule())
        consts = ctx.enter_context(tc.tile_pool(name="consts", bufs=1))
        products = ctx.enter_context(tc.tile_pool(name="products", bufs=BLOCKS))
        results = ctx.enter_context(tc.tile_pool(name="results", bufs=BLOCKS))
        psum = ctx.enter_context(tc.psum_pool(name="psum", bufs=8))

        x_sb = consts.tile([P, DIM], BF16)
        w_words = consts.tile([P, 2, 2 * FEATURES], U8, align_bytes=64)
        w_planes = consts.tile([P, 2, FEATURES], U8, align_bytes=64)
        position = consts.tile([P, 1], I32)
        identity = consts.tile([P, P], F32)
        nc.sync.dma_start(out=x_sb[:], in_=x.flatten_outer_dims())
        make_identity(nc, identity[:])
        idle = psum.tile([P, P], F32, tag="bank")

        def keep_busy(count):
            for unused in range(count):
                nc.tensor.matmul(out=idle[:], lhsT=identity[:], rhs=identity[:], start=True, stop=True)

        keep_busy(WARM_BEFORE)
        primed = consts.tile([P, 1], F32)
        nc.scalar.activation(out=primed[:], in_=identity[:, 0:1], func=ACT.Sin)
        load_words(nc, Wq_words, w_words[:, 0, :], 0, 1)
        nc.vector.memset(w_planes[:, 0, :].bitcast(I32), 0)
        load_scales(nc, Wq_scales, w_planes[:, 0, :])
        load_words(nc, Wq_words, w_words[:, 0, :], 1, BANKS)
        load_words(nc, Wk_words, w_words[:, 1, :], 0, BANKS)
        for s in range(SEQUENCES):
            nc.gpsimd.iota(
                position[s * POSITIONS : (s + 1) * POSITIONS, :], pattern=[[0, 1]], base=0, channel_multiplier=1
            )

        table = [P, 2, PAIRS, 2]
        freq = consts.tile(table, F32)
        phase = consts.tile(table, F32)
        position_turns = consts.tile([P, 1], F32)

        def spread_freq(known, copies):
            for j in range(1, copies + 1):
                nc.vector.tensor_scalar_mul(
                    out=freq[:, :, j * known : (j + 1) * known, :],
                    in0=freq[:, :, 0:known, :],
                    scalar1=RATIO ** (j * known),
                )

        nc.vector.memset(freq[:, :, 0:1, :], 1.0)
        nc.vector.memset(freq[:, 0:1, 0:1, 1:2], -1.0)
        nc.vector.memset(phase[:], 0.0)
        spread_freq(1, 3)
        nc.vector.memset(phase[:, 0:1, :, 0:1], 0.25)
        nc.vector.memset(phase[:, 1:2, :, 1:2], 0.25)
        spread_freq(4, 3)
        nc.vector.memset(w_planes[:, 1, :].bitcast(I32), 0)
        load_scales(nc, Wk_scales, w_planes[:, 1, :])
        spread_freq(16, 1)
        nc.vector.tensor_scalar_mul(out=position_turns[:], in0=position[:], scalar1=1.0 / (2.0 * math.pi))

        def flat(tile):
            return tile[:].rearrange("p e i k -> p (e i k)")

        turns = consts.tile(table, F32)
        nc.vector.scalar_tensor_tensor(
            out=flat(turns), in0=flat(freq), scalar=position_turns[:, 0:1], in1=flat(phase), op0=ALU.mult, op1=ALU.add
        )
        whole = consts.tile(table, F32)
        nc.vector.tensor_scalar(
            out=flat(whole), in0=flat(turns), scalar1=ROUND_MAGIC, scalar2=ROUND_MAGIC, op0=ALU.add, op1=ALU.subtract
        )

        x_pairs = x_sb[:].bitcast(F32)
        flipped = psum.tile([P, 2, P], F32, tag="bank")
        for u in range(2):
            nc.tensor.transpose(flipped[:, u, :], x_pairs[:, u : DIM // 2 : 2], identity[:])
        keep_busy(WARM_AFTER)
        part = consts.tile(table, F32)
        nc.vector.tensor_sub(out=flat(part), in0=flat(turns), in1=flat(whole))

        grouped = consts.tile([P, 4 * P], BF16, align_bytes=64)
        nc.scalar.copy(
            out=grouped[:].bitcast(F32).rearrange("p (r u) -> p r u", u=2),
            in_=flipped[:].rearrange("p u r -> p r u"),
        )
        rot = consts.tile(table, F32)
        nc.scalar.activation(out=flat(rot), in_=flat(part), func=ACT.Sin, scale=2.0 * math.pi)

        x_words = consts.tile([P, P], U32, align_bytes=64)
        x_plane = consts.tile([P, P], U8, align_bytes=64)
        nc.vector.quantize_mx(out=x_words[:].bitcast(FP8X4), scales=x_plane[:], in_=grouped[:])

        out_rows = [out.rearrange("b s h d -> (b s) (h d)") for out in (out_0, out_1)]
        wide = [P, 2, BANK_HEADS, 2 * PAIRS]

        def project(block, first_head, heads):
            w, c = divmod(block, BANKS)
            first = BANK_COLS * c + HEAD_DIM * first_head
            end = first + HEAD_DIM * heads
            acc = psum.tile([P, heads, HEAD_DIM], F32, tag="bank")
            nc.tensor.matmul_mx(
                out=acc[:].rearrange("p h d -> p (h d)"),
                lhsT=x_words[:].bitcast(FP8X4),
                lhsT_scale=x_plane[:],
                rhs=w_words[:, w, 2 * first : 2 * end].bitcast(FP4X4),
                rhs_scale=w_planes[:, w, first:end],
                start=True,
                stop=True,
            )
            return acc

        def multiply(acc, prod, heads):
            shape = [P, 2, heads, 2 * PAIRS]
            nc.vector.tensor_tensor(
                out=prod,
                in0=acc[:, :, PLAIN:HEAD_DIM].unsqueeze(1).to_broadcast(shape),
                in1=rot[:].rearrange("p e i k -> p e (i k)").unsqueeze(2).to_broadcast(shape),
                op=ALU.mult,
            )

        def sum_and_store(engine, block, prod, result, first_head=0, heads=BANK_HEADS):
            w, c = divmod(block, BANKS)
            mine = slice(first_head, first_head + heads)
            terms = prod[:, :, mine, :].rearrange("p e h (i k) -> p k h i e", k=2)
            engine.tensor_tensor(
                out=result[:, mine, PLAIN:HEAD_DIM].rearrange("p h (i e) -> p h i e", e=2),
                in0=terms[:, 0],
                in1=terms[:, 1],
                op=ALU.add,
            )
            first = BANK_COLS * c + HEAD_DIM * first_head
            nc.sync.dma_start(
                out=out_rows[w][:, first : first + HEAD_DIM * heads],
                in_=result[:, mine, :].rearrange("p h d -> p (h d)"),
            )

        owed = []
        for block in range(BLOCKS):
            prod = products.tile(wide, F32)
            result = results.tile([P, BANK_HEADS, HEAD_DIM], F32)
            if block == 0:
                heads = BANK_HEADS // FIRST_PIECES
                for piece in range(FIRST_PIECES):
                    mine = slice(heads * piece, heads * (piece + 1))
                    acc = project(block, heads * piece, heads)
                    multiply(acc, prod[:, :, mine, :], heads)
                    nc.scalar.copy(out=result[:, mine, 0:PLAIN], in_=acc[:, :, 0:PLAIN])
                    done = heads * (piece + 1)
                    if done % FIRST_SUM_HEADS == 0:
                        sum_and_store(nc.gpsimd, block, prod, result, done - FIRST_SUM_HEADS, FIRST_SUM_HEADS)
            elif block < BLOCKS - 1:
                acc = project(block, 0, BANK_HEADS)
                multiply(acc, prod[:], BANK_HEADS)
                nc.scalar.copy(out=result[:, :, 0:PLAIN], in_=acc[:, :, 0:PLAIN])
            if 0 < block < GPSIMD_SUMS:
                sum_and_store(nc.gpsimd, block, prod, result)
            elif GPSIMD_SUMS <= block < BLOCKS - 1:
                owed.append((block, prod, result))
            if block == VECTOR_SUMS_FROM:
                for late in owed:
                    sum_and_store(nc.vector, *late)
                owed.clear()
            if block == BLOCKS - 1:
                acc = project(block, 0, BANK_HEADS)
                nc.scalar.copy(out=result[:, :, 0:PLAIN], in_=acc[:, :, 0:PLAIN])
                heads = BANK_HEADS // LAST_PIECES
                for piece in range(LAST_PIECES):
                    mine = slice(heads * piece, heads * (piece + 1))
                    multiply(acc[:, mine, :], prod[:, :, mine, :], heads)
                for piece in range(LAST_PIECES):
                    sum_and_store(nc.vector, block, prod, result, heads * piece, heads)
